import numpy as np
import ml_dtypes


def mxq(x, axis, fmt="e4m3"):
    dtype, down = {"e4m3": (ml_dtypes.float8_e4m3fn, 7), "e5m2": (ml_dtypes.float8_e5m2, 14)}[fmt]
    v = np.moveaxis(np.asarray(x, np.float32).astype(ml_dtypes.bfloat16).astype(np.float64), axis, -1)
    blocks = v.reshape(v.shape[:-1] + (-1, 32))
    amax = np.abs(blocks).max(-1, keepdims=True)
    byte = np.maximum(np.where(amax > 0, np.frexp(amax)[1] - 1 + 127, 0) - down, 1)
    scale = np.exp2(byte - 127.0)
    codes = (blocks / scale).astype(np.float32).astype(dtype).astype(np.float64)
    return np.moveaxis((codes * scale).reshape(v.shape), -1, axis)


WIDE = False


def mx_kscale(k):
    if not WIDE:
        return np.ones(k)
    levels = np.array([10, -10, 5, -5, 0])
    if k % 512:
        return np.exp2(np.random.permutation(np.resize(levels, k // 32))).repeat(32)
    a = np.empty((k // 512, 16))
    for p in range(k // 512):
        a[p, :8] = np.random.permutation(np.resize(levels, 8))
        for g in range(8):
            far = levels[np.abs(levels - a[p, g]) >= 10]
            a[p, g + 8] = far[np.random.randint(len(far))]
    return np.exp2(a.ravel()).repeat(32)


BF16 = ml_dtypes.bfloat16


def bf(x):
    return np.asarray(x, np.float32).astype(BF16)


def f64(x):
    return np.asarray(x).astype(np.float64)


E, F, H, MID, OUT = 128, 128, 384, 1024, 128
D = 2 * (F + H)
IN = D + 1


def setup_inputs():
    s = mx_kscale(D)
    t = mx_kscale(MID)
    w1 = np.concatenate([np.random.standard_normal((MID, D)) / np.sqrt(D) / s[None, :],
                         np.random.standard_normal((MID, 1)) * 0.5], axis=1) * t[:, None]
    return {"dst_node_feat": bf(np.random.standard_normal((E, F)) * s[:F]),
            "dst_node_hidden": bf(np.random.standard_normal((E, H)) * s[F:F + H]),
            "src_node_feat": bf(np.random.standard_normal((E, F)) * s[F + H:2 * F + H]),
            "src_node_hidden": bf(np.random.standard_normal((E, H)) * s[2 * F + H:]),
            "edge_feat": bf(np.random.standard_normal(E)),
            "W1": bf(w1),
            "b1": bf(np.random.standard_normal(MID) * 0.3 * t),
            "W2": bf(np.random.standard_normal((OUT, MID)) / np.sqrt(MID) / t[None, :]),
            "b2": bf(np.random.standard_normal(OUT) * 0.3)}


def reference(dst_node_feat, dst_node_hidden, src_node_feat, src_node_hidden, edge_feat, W1, b1, W2, b2):
    x = np.concatenate([f64(dst_node_feat), f64(dst_node_hidden), f64(src_node_feat), f64(src_node_hidden),
                        f64(edge_feat)[:, None]], axis=1)
    w1 = f64(W1)
    pre = (mxq(x[:, :D], 1, "e4m3") @ mxq(w1[:, :D], 1, "e4m3").T) + x[:, D:] * w1[:, D] + f64(b1)
    h = np.maximum(pre, 0.0)
    return np.tanh((mxq(h, 1, "e4m3") @ mxq(f64(W2), 1, "e4m3").T) + f64(b2))

@@ -1,0 +1,212 @@
+from contextlib import ExitStack
+
+import concourse.mybir as mybir
+from concourse.masks import make_identity
+
+F32 = mybir.dt.float32
+BF16 = mybir.dt.bfloat16
+U32 = mybir.dt.uint32
+U8 = mybir.dt.uint8
+FP8X4 = mybir.dt.float8_e4m3fn_x4
+ALU = mybir.AluOpType
+ACT = mybir.ActivationFunctionType
+
+P = 128
+PACK = 4
+K_PASS = P * PACK
+NODE = 1024
+MID = 1024
+PASSES = NODE // K_PASS
+HALVES = 2
+BLOCKS = MID // P
+PAIRS = BLOCKS // 2
+W2_STEP = PAIRS // 2
+
+FLOPS = 2 * P * (NODE + 1) * MID + 2 * P * MID * P
+
+
+def tile_edgenetwork_s_kernel(
+    tc,
+    dst_node_feat,
+    dst_node_hidden,
+    src_node_feat,
+    src_node_hidden,
+    edge_feat,
+    W1,
+    b1,
+    W2,
+    b2,
+    out,
+):
+    nc = tc.nc
+    with ExitStack() as ctx:
+        keep = ctx.enter_context(tc.tile_pool(name="keep", bufs=1))
+        w1_pool = ctx.enter_context(tc.tile_pool(name="w1", bufs=BLOCKS))
+        stream = ctx.enter_context(tc.tile_pool(name="stream", bufs=6))
+        flip_banks = ctx.enter_context(tc.psum_pool(name="flip", bufs=4))
+        hidden_banks = ctx.enter_context(tc.psum_pool(name="hidden", bufs=2))
+        single_banks = ctx.enter_context(tc.psum_pool(name="single", bufs=1))
+        ctx.enter_context(tc.manual_schedule())
+
+        identity = keep.tile([P, P], F32)
+        make_identity(nc, identity[:])
+        vectors = keep.tile([P, 6 * P], BF16)
+        nc.vector.memset(vectors[:], 0.0)
+        ones = keep.tile([P, P], BF16)
+        nc.vector.memset(ones[:], 1.0)
+        table_in = keep.tile([P, 1], F32)
+        table_out = keep.tile([P, 1], F32)
+        nc.vector.memset(table_in[:], 0.0)
+        nc.scalar.activation(out=table_out[:], in_=table_in[:], func=ACT.Tanh)
+
+        x_rows = keep.tile([P, NODE], BF16)
+        column = 0
+        for part in (dst_node_feat, dst_node_hidden, src_node_feat, src_node_hidden):
+            width = part.shape[1]
+            nc.sync.dma_start(out=x_rows[:, column : column + width], in_=part)
+            column += width
+
+        w1_blocks = W1.rearrange("(c p t) k -> c t p k", p=P, t=PACK)
+        w2_rows = keep.tile([P, MID], BF16)
+        w1_rows = []
+        for block in range(BLOCKS):
+            if block == 2 * W2_STEP:
+                nc.sync.dma_start(out=w2_rows[:], in_=W2)
+            rows = w1_pool.tile([P, NODE + 2], BF16, name="w1_rows")
+            nc.sync.dma_start(out=rows[:, 0 : NODE + 1], in_=w1_blocks[block // PACK, block % PACK])
+            w1_rows.append(rows)
+
+        nc.gpsimd.dma_start(out=vectors[0:1, 4 * P : 5 * P], in_=edge_feat.rearrange("(o e) -> o e", o=1))
+        nc.gpsimd.dma_start(out=vectors[0:PASSES, 0 : 4 * P], in_=b1.rearrange("(c q) -> c q", q=4 * P))
+        nc.gpsimd.dma_start(out=vectors[0:1, 5 * P : 6 * P], in_=b2.rearrange("(o n) -> o n", o=1))
+
+        def flip(rows):
+            words = rows[:, 0:NODE].bitcast(F32)
+            bank = flip_banks.tile([P, PASSES * HALVES, P], F32)
+            for q in range(PASSES * HALVES):
+                g, u = divmod(q, HALVES)
+                first = g * HALVES * P + u
+                nc.tensor.transpose(bank[:, q, :], words[:, first : (g + 1) * HALVES * P : HALVES], identity[:])
+            grouped = stream.tile([P, PASSES, P, PACK], BF16, align_bytes=64)
+            nc.scalar.copy(
+                out=grouped[:].bitcast(F32),
+                in_=bank[:].rearrange("p (g u) c -> p g c u", u=HALVES),
+            )
+            return grouped
+
+        def quantise(grouped, pool, name):
+            codes = pool.tile([P, PASSES * P], U32, name=name + "_codes", align_bytes=64)
+            scales = pool.tile([P, PASSES * P], U8, name=name + "_scales", align_bytes=64)
+            nc.vector.quantize_mx(
+                out=codes[:].bitcast(FP8X4),
+                scales=scales[:],
+                in_=grouped[:].rearrange("p g c t -> p (g c t)"),
+            )
+            return codes, scales
+
+        def multiply(pair):
+            operands = [quantise(turned_w1[2 * pair + r], stream, "w1") for r in range(2)]
+            acc = hidden_banks.tile([P, 2, P], F32, name="hidden_acc")
+            for r in range(2):
+                w1_codes, w1_scales = operands[r]
+                for g in range(PASSES):
+                    cols = slice(g * P, (g + 1) * P)
+                    nc.tensor.matmul_mx(
+                        out=acc[:, r, :],
+                        lhsT=w1_codes[:, cols].bitcast(FP8X4),
+                        lhsT_scale=w1_scales[:, cols],
+                        rhs=x_codes[:, cols].bitcast(FP8X4),
+                        rhs_scale=x_scales[:, cols],
+                        start=(g == 0),
+                        stop=(g == PASSES - 1),
+                    )
+            hidden_acc[pair] = acc
+
+        def spread_vectors():
+            bank = single_banks.tile([P, 4 * P], F32, name="vector_bank")
+            b1_words = vectors[:, 0 : 4 * P].bitcast(F32)
+            for u in range(HALVES):
+                nc.tensor.transpose(bank[:, u * P : (u + 1) * P], b1_words[:, u : HALVES * P : HALVES], identity[:])
+            nc.tensor.matmul(out=bank[:, 2 * P : 4 * P], lhsT=ones[:], rhs=vectors[:, 4 * P : 6 * P], start=True, stop=True)
+            for u in range(HALVES):
+                nc.vector.tensor_copy(
+                    out=b1_cols[:].rearrange("p (c u e) -> p u c e", c=PASSES, u=HALVES)[:, u],
+                    in_=bank[:, u * P : u * P + PASSES].bitcast(BF16).rearrange("p (c e) -> p c e", c=PASSES),
+                )
+            nc.vector.tensor_copy(out=spread[:], in_=bank[:, 2 * P : 4 * P])
+
+        def activate(pair):
+            c, u = divmod(pair, HALVES)
+            sums = []
+            for r in range(2):
+                pre = stream.tile([P, P], F32, name="pre")
+                nc.vector.scalar_tensor_tensor(
+                    out=pre[:],
+                    in0=spread[:, 0:P],
+                    scalar=w1_rows[2 * pair + r][:, NODE : NODE + 1],
+                    in1=hidden_acc[pair][:, r, :],
+                    op0=ALU.mult,
+                    op1=ALU.add,
+                )
+                sums.append(pre)
+            for r in range(2):
+                block = 2 * pair + r
+                nc.vector.tensor_scalar(
+                    out=h_grouped[:, c, :, HALVES * u + r],
+                    in0=sums[r][:],
+                    scalar1=b1_cols[:, block : block + 1],
+                    scalar2=0.0,
+                    op0=ALU.add,
+                    op1=ALU.max,
+                )
+
+        def second_layer_pass(c):
+            cols = slice(c * P, (c + 1) * P)
+            nc.vector.quantize_mx(
+                out=h_codes[:, cols].bitcast(FP8X4),
+                scales=h_scales[:, cols],
+                in_=h_grouped[:, c, :, :].rearrange("p e t -> p (e t)"),
+            )
+            nc.tensor.matmul_mx(
+                out=out_acc[:],
+                lhsT=h_codes[:, cols].bitcast(FP8X4),
+                lhsT_scale=h_scales[:, cols],
+                rhs=w2_codes[:, cols].bitcast(FP8X4),
+                rhs_scale=w2_scales[:, cols],
+                start=(c == 0),
+                stop=(c == PASSES - 1),
+            )
+
+        b1_cols = keep.tile([P, BLOCKS], F32)
+        spread = keep.tile([P, 2 * P], F32)
+        h_grouped = keep.tile([P, PASSES, P, PACK], BF16, align_bytes=64)
+        h_codes = keep.tile([P, PASSES * P], U32, align_bytes=64)
+        h_scales = keep.tile([P, PASSES * P], U8, align_bytes=64)
+        out_acc = single_banks.tile([P, P], F32)
+        turned_w1 = {}
+        hidden_acc = {}
+
+        x_codes, x_scales = quantise(flip(x_rows), keep, "x")
+
+        for step in range(PAIRS + 2):
+            if step == W2_STEP:
+                turned_w2 = flip(w2_rows)
+            if step < PAIRS:
+                for r in range(2):
+                    turned_w1[2 * step + r] = flip(w1_rows[2 * step + r])
+            if 1 <= step <= PAIRS:
+                multiply(step - 1)
+            if step == 1:
+                spread_vectors()
+            if step >= 2:
+                activate(step - 2)
+                if (step - 2) % HALVES == HALVES - 1:
+                    second_layer_pass((step - 2) // HALVES)
+            if step == W2_STEP:
+                w2_codes, w2_scales = quantise(turned_w2, keep, "w2")
+
+        biased = keep.tile([P, P], F32)
+        nc.vector.tensor_tensor(out=biased[:], in0=out_acc[:], in1=spread[:, P : 2 * P], op=ALU.add)
+        result = keep.tile([P, P], F32)
+        nc.scalar.activation(out=result[:], in_=biased[:], func=ACT.Tanh)
+        nc.sync.dma_start(out=out, in_=result[:])

@@ -19,8 +19,7 @@ MID = 1024
 PASSES = NODE // K_PASS
 HALVES = 2
 BLOCKS = MID // P
-PAIRS = BLOCKS // 2
-W2_STEP = PAIRS // 2
+LAST = BLOCKS - 1
 
 FLOPS = 2 * P * (NODE + 1) * MID + 2 * P * MID * P
 
@@ -41,23 +40,20 @@ def tile_edgenetwork_s_kernel(
     nc = tc.nc
     with ExitStack() as ctx:
         keep = ctx.enter_context(tc.tile_pool(name="keep", bufs=1))
-        w1_pool = ctx.enter_context(tc.tile_pool(name="w1", bufs=BLOCKS))
-        stream = ctx.enter_context(tc.tile_pool(name="stream", bufs=6))
+        blocks = ctx.enter_context(tc.tile_pool(name="blocks", bufs=BLOCKS + 2))
         flip_banks = ctx.enter_context(tc.psum_pool(name="flip", bufs=4))
-        hidden_banks = ctx.enter_context(tc.psum_pool(name="hidden", bufs=2))
-        single_banks = ctx.enter_context(tc.psum_pool(name="single", bufs=1))
+        banks = ctx.enter_context(tc.psum_pool(name="banks", bufs=1))
         ctx.enter_context(tc.manual_schedule())
 
+        vectors = keep.tile([P, 2 * P], BF16)
+        nc.vector.memset(vectors[:], 0.0)
         identity = keep.tile([P, P], F32)
         make_identity(nc, identity[:])
-        vectors = keep.tile([P, 6 * P], BF16)
-        nc.vector.memset(vectors[:], 0.0)
         ones = keep.tile([P, P], BF16)
         nc.vector.memset(ones[:], 1.0)
         table_in = keep.tile([P, 1], F32)
         table_out = keep.tile([P, 1], F32)
         nc.vector.memset(table_in[:], 0.0)
-        nc.scalar.activation(out=table_out[:], in_=table_in[:], func=ACT.Tanh)
 
         x_rows = keep.tile([P, NODE], BF16)
         column = 0
@@ -66,109 +62,121 @@ def tile_edgenetwork_s_kernel(
             nc.sync.dma_start(out=x_rows[:, column : column + width], in_=part)
             column += width
 
+        b1_cols = keep.tile([P, PASSES, PACK], BF16)
+        nc.scalar.dma_start(out=b1_cols[:], in_=b1.rearrange("(c p t) -> p c t", p=P, t=PACK))
+        nc.scalar.dma_start(out=vectors[0:1, 0:P], in_=edge_feat.rearrange("(o e) -> o e", o=1))
+        nc.scalar.activation(out=table_out[:], in_=table_in[:], func=ACT.Tanh)
+
         w1_blocks = W1.rearrange("(c p t) k -> c t p k", p=P, t=PACK)
-        w2_rows = keep.tile([P, MID], BF16)
         w1_rows = []
         for block in range(BLOCKS):
-            if block == 2 * W2_STEP:
-                nc.sync.dma_start(out=w2_rows[:], in_=W2)
-            rows = w1_pool.tile([P, NODE + 2], BF16, name="w1_rows")
+            rows = blocks.tile([P, NODE + 2], BF16, name="w1_rows")
             nc.sync.dma_start(out=rows[:, 0 : NODE + 1], in_=w1_blocks[block // PACK, block % PACK])
             w1_rows.append(rows)
+            if block == 1:
+                nc.sync.dma_start(out=vectors[0:1, P : 2 * P], in_=b2.rearrange("(o n) -> o n", o=1))
+        w2_rows = keep.tile([P, MID], BF16)
+        nc.sync.dma_start(out=w2_rows[:], in_=W2)
 
-        nc.gpsimd.dma_start(out=vectors[0:1, 4 * P : 5 * P], in_=edge_feat.rearrange("(o e) -> o e", o=1))
-        nc.gpsimd.dma_start(out=vectors[0:PASSES, 0 : 4 * P], in_=b1.rearrange("(c q) -> c q", q=4 * P))
-        nc.gpsimd.dma_start(out=vectors[0:1, 5 * P : 6 * P], in_=b2.rearrange("(o n) -> o n", o=1))
+        turned = {}
+        operands = {}
+        edge_terms = keep.tile([P, BLOCKS, P], F32)
+        spread = keep.tile([P, 2 * P], F32)
+        pre = keep.tile([P, BLOCKS, P], F32)
+        h_grouped = keep.tile([P, PASSES, P, PACK], BF16, align_bytes=64)
+        h_codes = keep.tile([P, PASSES * P], U32, align_bytes=64)
+        h_scales = keep.tile([P, PASSES * P], U8, align_bytes=64)
+        hidden_first = banks.tile([P, PACK, P], F32)
+        hidden_rest = banks.tile([P, PACK - 1, P], F32)
+        hidden_last = banks.tile([P, 1, P], F32)
+        misc = banks.tile([P, 3 * P], F32)
+        out_acc = misc[:, 2 * P : 3 * P]
 
-        def flip(rows):
+        def flip(key, rows):
             words = rows[:, 0:NODE].bitcast(F32)
             bank = flip_banks.tile([P, PASSES * HALVES, P], F32)
             for q in range(PASSES * HALVES):
                 g, u = divmod(q, HALVES)
                 first = g * HALVES * P + u
                 nc.tensor.transpose(bank[:, q, :], words[:, first : (g + 1) * HALVES * P : HALVES], identity[:])
-            grouped = stream.tile([P, PASSES, P, PACK], BF16, align_bytes=64)
+            grouped = blocks.tile([P, PASSES, P, PACK], BF16, align_bytes=64)
             nc.scalar.copy(
                 out=grouped[:].bitcast(F32),
                 in_=bank[:].rearrange("p (g u) c -> p g c u", u=HALVES),
             )
-            return grouped
+            turned[key] = grouped
 
-        def quantise(grouped, pool, name):
-            codes = pool.tile([P, PASSES * P], U32, name=name + "_codes", align_bytes=64)
-            scales = pool.tile([P, PASSES * P], U8, name=name + "_scales", align_bytes=64)
+        def quantise(key):
+            codes = blocks.tile([P, PASSES * P], U32, align_bytes=64)
+            scales = blocks.tile([P, PASSES * P], U8, align_bytes=64)
             nc.vector.quantize_mx(
                 out=codes[:].bitcast(FP8X4),
                 scales=scales[:],
-                in_=grouped[:].rearrange("p g c t -> p (g c t)"),
+                in_=turned[key][:].rearrange("p g c t -> p (g c t)"),
             )
-            return codes, scales
+            operands[key] = (codes, scales)
 
-        def multiply(pair):
-            operands = [quantise(turned_w1[2 * pair + r], stream, "w1") for r in range(2)]
-            acc = hidden_banks.tile([P, 2, P], F32, name="hidden_acc")
-            for r in range(2):
-                w1_codes, w1_scales = operands[r]
-                for g in range(PASSES):
-                    cols = slice(g * P, (g + 1) * P)
-                    nc.tensor.matmul_mx(
-                        out=acc[:, r, :],
-                        lhsT=w1_codes[:, cols].bitcast(FP8X4),
-                        lhsT_scale=w1_scales[:, cols],
-                        rhs=x_codes[:, cols].bitcast(FP8X4),
-                        rhs_scale=x_scales[:, cols],
-                        start=(g == 0),
-                        stop=(g == PASSES - 1),
-                    )
-            hidden_acc[pair] = acc
-
-        def spread_vectors():
-            bank = single_banks.tile([P, 4 * P], F32, name="vector_bank")
-            b1_words = vectors[:, 0 : 4 * P].bitcast(F32)
-            for u in range(HALVES):
-                nc.tensor.transpose(bank[:, u * P : (u + 1) * P], b1_words[:, u : HALVES * P : HALVES], identity[:])
-            nc.tensor.matmul(out=bank[:, 2 * P : 4 * P], lhsT=ones[:], rhs=vectors[:, 4 * P : 6 * P], start=True, stop=True)
-            for u in range(HALVES):
-                nc.vector.tensor_copy(
-                    out=b1_cols[:].rearrange("p (c u e) -> p u c e", c=PASSES, u=HALVES)[:, u],
-                    in_=bank[:, u * P : u * P + PASSES].bitcast(BF16).rearrange("p (c e) -> p c e", c=PASSES),
-                )
-            nc.vector.tensor_copy(out=spread[:], in_=bank[:, 2 * P : 4 * P])
-
-        def activate(pair):
-            c, u = divmod(pair, HALVES)
-            sums = []
-            for r in range(2):
-                pre = stream.tile([P, P], F32, name="pre")
-                nc.vector.scalar_tensor_tensor(
-                    out=pre[:],
-                    in0=spread[:, 0:P],
-                    scalar=w1_rows[2 * pair + r][:, NODE : NODE + 1],
-                    in1=hidden_acc[pair][:, r, :],
-                    op0=ALU.mult,
-                    op1=ALU.add,
-                )
-                sums.append(pre)
-            for r in range(2):
-                block = 2 * pair + r
-                nc.vector.tensor_scalar(
-                    out=h_grouped[:, c, :, HALVES * u + r],
-                    in0=sums[r][:],
-                    scalar1=b1_cols[:, block : block + 1],
-                    scalar2=0.0,
-                    op0=ALU.add,
-                    op1=ALU.max,
+        def multiply(block):
+            if block < PACK:
+                acc = hidden_first[:, block, :]
+            elif block < LAST:
+                acc = hidden_rest[:, block - PACK, :]
+            else:
+                acc = hidden_last[:, 0, :]
+            w1_codes, w1_scales = operands[block]
+            x_codes, x_scales = operands["x"]
+            for g in range(PASSES):
+                cols = slice(g * P, (g + 1) * P)
+                nc.tensor.matmul_mx(
+                    out=acc,
+                    lhsT=w1_codes[:, cols].bitcast(FP8X4),
+                    lhsT_scale=w1_scales[:, cols],
+                    rhs=x_codes[:, cols].bitcast(FP8X4),
+                    rhs_scale=x_scales[:, cols],
+                    start=(g == 0),
+                    stop=(g == PASSES - 1),
                 )
 
-        def second_layer_pass(c):
+        def edge_term(block):
+            nc.vector.tensor_scalar(
+                out=edge_terms[:, block, :],
+                in0=spread[:, 0:P],
+                scalar1=w1_rows[block][:, NODE : NODE + 1],
+                scalar2=b1_cols[:, block // PACK, block % PACK : block % PACK + 1],
+                op0=ALU.mult,
+                op1=ALU.add,
+            )
+
+        def add_edge_terms(acc, first, last):
+            nc.vector.tensor_tensor(
+                out=pre[:, first:last, :],
+                in0=acc,
+                in1=edge_terms[:, first:last, :],
+                op=ALU.add,
+            )
+
+        def relu(c):
+            nc.vector.tensor_scalar(
+                out=h_grouped[:, c, :, :],
+                in0=pre[:, c * PACK : (c + 1) * PACK, :].rearrange("p t e -> p e t"),
+                scalar1=0.0,
+                scalar2=None,
+                op0=ALU.max,
+            )
+
+        def quantise_hidden(c):
             cols = slice(c * P, (c + 1) * P)
             nc.vector.quantize_mx(
                 out=h_codes[:, cols].bitcast(FP8X4),
                 scales=h_scales[:, cols],
                 in_=h_grouped[:, c, :, :].rearrange("p e t -> p (e t)"),
             )
+
+        def second_layer(c):
+            w2_codes, w2_scales = operands["w2"]
+            cols = slice(c * P, (c + 1) * P)
             nc.tensor.matmul_mx(
-                out=out_acc[:],
+                out=out_acc,
                 lhsT=h_codes[:, cols].bitcast(FP8X4),
                 lhsT_scale=h_scales[:, cols],
                 rhs=w2_codes[:, cols].bitcast(FP8X4),
@@ -177,36 +185,48 @@ def tile_edgenetwork_s_kernel(
                 stop=(c == PASSES - 1),
             )
 
-        b1_cols = keep.tile([P, BLOCKS], F32)
-        spread = keep.tile([P, 2 * P], F32)
-        h_grouped = keep.tile([P, PASSES, P, PACK], BF16, align_bytes=64)
-        h_codes = keep.tile([P, PASSES * P], U32, align_bytes=64)
-        h_scales = keep.tile([P, PASSES * P], U8, align_bytes=64)
-        out_acc = single_banks.tile([P, P], F32)
-        turned_w1 = {}
-        hidden_acc = {}
-
-        x_codes, x_scales = quantise(flip(x_rows), keep, "x")
-
-        for step in range(PAIRS + 2):
-            if step == W2_STEP:
-                turned_w2 = flip(w2_rows)
-            if step < PAIRS:
-                for r in range(2):
-                    turned_w1[2 * step + r] = flip(w1_rows[2 * step + r])
-            if 1 <= step <= PAIRS:
-                multiply(step - 1)
-            if step == 1:
-                spread_vectors()
-            if step >= 2:
-                activate(step - 2)
-                if (step - 2) % HALVES == HALVES - 1:
-                    second_layer_pass((step - 2) // HALVES)
-            if step == W2_STEP:
-                w2_codes, w2_scales = quantise(turned_w2, keep, "w2")
+        flip("x", x_rows)
+        flip(0, w1_rows[0])
+        quantise("x")
+        flip(1, w1_rows[1])
+        quantise(0)
+        flip(2, w1_rows[2])
+        quantise(1)
+        flip(3, w1_rows[3])
+        quantise(2)
+        nc.tensor.matmul(out=misc[:, 0 : 2 * P], lhsT=ones[:], rhs=vectors[:], start=True, stop=True)
+        nc.vector.tensor_copy(out=spread[:], in_=misc[:, 0 : 2 * P])
+        flip(4, w1_rows[4])
+        quantise(3)
+        for block in range(PACK):
+            edge_term(block)
+        for block in range(PACK):
+            multiply(block)
+        flip(5, w1_rows[5])
+        quantise(4)
+        add_edge_terms(hidden_first[:], 0, PACK)
+        flip(6, w1_rows[6])
+        quantise(5)
+        relu(0)
+        flip(7, w1_rows[7])
+        quantise(6)
+        quantise_hidden(0)
+        flip("w2", w2_rows)
+        for block in range(PACK, BLOCKS):
+            edge_term(block)
+        quantise(7)
+        for block in range(PACK, BLOCKS):
+            multiply(block)
+        add_edge_terms(hidden_rest[:], PACK, LAST)
+        add_edge_terms(hidden_last[:], LAST, BLOCKS)
+        quantise("w2")
+        relu(1)
+        quantise_hidden(1)
+        second_layer(0)
+        second_layer(1)
 
         biased = keep.tile([P, P], F32)
-        nc.vector.tensor_tensor(out=biased[:], in0=out_acc[:], in1=spread[:, P : 2 * P], op=ALU.add)
+        nc.vector.tensor_tensor(out=biased[:], in0=out_acc, in1=spread[:, P : 2 * P], op=ALU.add)
         result = keep.tile([P, P], F32)
         nc.scalar.activation(out=result[:], in_=biased[:], func=ACT.Tanh)
         nc.sync.dma_start(out=out, in_=result[:])

@@ -45,7 +45,7 @@ def tile_edgenetwork_s_kernel(
         banks = ctx.enter_context(tc.psum_pool(name="banks", bufs=1))
         ctx.enter_context(tc.manual_schedule())
 
-        vectors = keep.tile([P, 2 * P], BF16)
+        vectors = keep.tile([P, 6 * P], BF16)
         nc.vector.memset(vectors[:], 0.0)
         identity = keep.tile([P, P], F32)
         make_identity(nc, identity[:])
@@ -62,9 +62,8 @@ def tile_edgenetwork_s_kernel(
             nc.sync.dma_start(out=x_rows[:, column : column + width], in_=part)
             column += width
 
-        b1_cols = keep.tile([P, PASSES, PACK], BF16)
-        nc.scalar.dma_start(out=b1_cols[:], in_=b1.rearrange("(c p t) -> p c t", p=P, t=PACK))
-        nc.scalar.dma_start(out=vectors[0:1, 0:P], in_=edge_feat.rearrange("(o e) -> o e", o=1))
+        nc.scalar.dma_start(out=vectors[0:PASSES, 0:K_PASS], in_=b1.rearrange("(c q) -> c q", q=K_PASS))
+        nc.scalar.dma_start(out=vectors[0:1, 4 * P : 5 * P], in_=edge_feat.rearrange("(o e) -> o e", o=1))
         nc.scalar.activation(out=table_out[:], in_=table_in[:], func=ACT.Tanh)
 
         w1_blocks = W1.rearrange("(c p t) k -> c t p k", p=P, t=PACK)
@@ -74,13 +73,14 @@ def tile_edgenetwork_s_kernel(
             nc.sync.dma_start(out=rows[:, 0 : NODE + 1], in_=w1_blocks[block // PACK, block % PACK])
             w1_rows.append(rows)
             if block == 1:
-                nc.sync.dma_start(out=vectors[0:1, P : 2 * P], in_=b2.rearrange("(o n) -> o n", o=1))
+                nc.sync.dma_start(out=vectors[0:1, 5 * P : 6 * P], in_=b2.rearrange("(o n) -> o n", o=1))
         w2_rows = keep.tile([P, MID], BF16)
         nc.sync.dma_start(out=w2_rows[:], in_=W2)
 
         turned = {}
         operands = {}
         edge_terms = keep.tile([P, BLOCKS, P], F32)
+        b1_cols = keep.tile([P, PASSES, PACK], BF16)
         spread = keep.tile([P, 2 * P], F32)
         pre = keep.tile([P, BLOCKS, P], F32)
         h_grouped = keep.tile([P, PASSES, P, PACK], BF16, align_bytes=64)
@@ -89,10 +89,9 @@ def tile_edgenetwork_s_kernel(
         hidden_first = banks.tile([P, PACK, P], F32)
         hidden_rest = banks.tile([P, PACK - 1, P], F32)
         hidden_last = banks.tile([P, 1, P], F32)
-        misc = banks.tile([P, 3 * P], F32)
-        out_acc = misc[:, 2 * P : 3 * P]
+        out_acc = banks.tile([P, P], F32)
 
-        def flip(key, rows):
+        def flip(key, rows, copy=nc.scalar.copy):
             words = rows[:, 0:NODE].bitcast(F32)
             bank = flip_banks.tile([P, PASSES * HALVES, P], F32)
             for q in range(PASSES * HALVES):
@@ -100,7 +99,7 @@ def tile_edgenetwork_s_kernel(
                 first = g * HALVES * P + u
                 nc.tensor.transpose(bank[:, q, :], words[:, first : (g + 1) * HALVES * P : HALVES], identity[:])
             grouped = blocks.tile([P, PASSES, P, PACK], BF16, align_bytes=64)
-            nc.scalar.copy(
+            copy(
                 out=grouped[:].bitcast(F32),
                 in_=bank[:].rearrange("p (g u) c -> p g c u", u=HALVES),
             )
@@ -176,7 +175,7 @@ def tile_edgenetwork_s_kernel(
             w2_codes, w2_scales = operands["w2"]
             cols = slice(c * P, (c + 1) * P)
             nc.tensor.matmul_mx(
-                out=out_acc,
+                out=out_acc[:],
                 lhsT=h_codes[:, cols].bitcast(FP8X4),
                 lhsT_scale=h_scales[:, cols],
                 rhs=w2_codes[:, cols].bitcast(FP8X4),
@@ -185,34 +184,49 @@ def tile_edgenetwork_s_kernel(
                 stop=(c == PASSES - 1),
             )
 
-        flip("x", x_rows)
+        def spread_vectors():
+            bank = flip_banks.tile([P, 4 * P], F32)
+            b1_words = vectors[:, 0:K_PASS].bitcast(F32)
+            for u in range(HALVES):
+                nc.tensor.transpose(bank[:, u * P : (u + 1) * P], b1_words[:, u : HALVES * P : HALVES], identity[:])
+            nc.tensor.matmul(out=bank[:, 2 * P : 4 * P], lhsT=ones[:], rhs=vectors[:, K_PASS:], start=True, stop=True)
+            for u in range(HALVES):
+                nc.scalar.copy(
+                    out=b1_cols[:].rearrange("p c (u e) -> p u c e", u=HALVES)[:, u],
+                    in_=bank[:, u * P : u * P + PASSES].bitcast(BF16).rearrange("p (c e) -> p c e", c=PASSES),
+                )
+            nc.scalar.copy(out=spread[:], in_=bank[:, 2 * P : 4 * P])
+
+        flip("x", x_rows, nc.vector.tensor_copy)
         flip(0, w1_rows[0])
         quantise("x")
         flip(1, w1_rows[1])
         quantise(0)
         flip(2, w1_rows[2])
+        spread_vectors()
         quantise(1)
         flip(3, w1_rows[3])
         quantise(2)
-        nc.tensor.matmul(out=misc[:, 0 : 2 * P], lhsT=ones[:], rhs=vectors[:], start=True, stop=True)
-        nc.vector.tensor_copy(out=spread[:], in_=misc[:, 0 : 2 * P])
+        edge_term(0)
+        edge_term(1)
         flip(4, w1_rows[4])
+        edge_term(2)
         quantise(3)
-        for block in range(PACK):
-            edge_term(block)
+        edge_term(3)
+        flip(5, w1_rows[5])
         for block in range(PACK):
             multiply(block)
-        flip(5, w1_rows[5])
         quantise(4)
-        add_edge_terms(hidden_first[:], 0, PACK)
         flip(6, w1_rows[6])
+        edge_term(4)
+        add_edge_terms(hidden_first[:], 0, PACK)
         quantise(5)
-        relu(0)
         flip(7, w1_rows[7])
+        relu(0)
         quantise(6)
         quantise_hidden(0)
         flip("w2", w2_rows)
-        for block in range(PACK, BLOCKS):
+        for block in range(PACK + 1, BLOCKS):
             edge_term(block)
         quantise(7)
         for block in range(PACK, BLOCKS):
@@ -226,7 +240,7 @@ def tile_edgenetwork_s_kernel(
         second_layer(1)
 
         biased = keep.tile([P, P], F32)
-        nc.vector.tensor_tensor(out=biased[:], in0=out_acc, in1=spread[:, P : 2 * P], op=ALU.add)
+        nc.vector.tensor_tensor(out=biased[:], in0=out_acc[:], in1=spread[:, P : 2 * P], op=ALU.add)
         result = keep.tile([P, P], F32)
         nc.scalar.activation(out=result[:], in_=biased[:], func=ACT.Tanh)
         nc.sync.dma_start(out=out, in_=result[:])

@@ -46,14 +46,14 @@ def tile_edgenetwork_s_kernel(
         ctx.enter_context(tc.manual_schedule())
 
         vectors = keep.tile([P, 6 * P], BF16)
-        nc.vector.memset(vectors[:], 0.0)
-        identity = keep.tile([P, P], F32)
-        make_identity(nc, identity[:])
-        ones = keep.tile([P, P], BF16)
-        nc.vector.memset(ones[:], 1.0)
+        nc.vector.memset(vectors[:].bitcast(U32), 0)
         table_in = keep.tile([P, 1], F32)
         table_out = keep.tile([P, 1], F32)
         nc.vector.memset(table_in[:], 0.0)
+        ones = keep.tile([P, P], BF16)
+        nc.vector.memset(ones[:], 1.0)
+        identity = keep.tile([P, P], F32)
+        make_identity(nc, identity[:])
 
         x_rows = keep.tile([P, NODE], BF16)
         column = 0
@@ -62,7 +62,8 @@ def tile_edgenetwork_s_kernel(
             nc.sync.dma_start(out=x_rows[:, column : column + width], in_=part)
             column += width
 
-        nc.scalar.dma_start(out=vectors[0:PASSES, 0:K_PASS], in_=b1.rearrange("(c q) -> c q", q=K_PASS))
+        nc.gpsimd.dma_start(out=vectors[0:PASSES, 0:K_PASS], in_=b1.rearrange("(c q) -> c q", q=K_PASS))
+        nc.gpsimd.dma_start(out=vectors[0:1, 5 * P : 6 * P], in_=b2.rearrange("(o n) -> o n", o=1))
         nc.scalar.dma_start(out=vectors[0:1, 4 * P : 5 * P], in_=edge_feat.rearrange("(o e) -> o e", o=1))
         nc.scalar.activation(out=table_out[:], in_=table_in[:], func=ACT.Tanh)
 
@@ -72,8 +73,6 @@ def tile_edgenetwork_s_kernel(
             rows = blocks.tile([P, NODE + 2], BF16, name="w1_rows")
             nc.sync.dma_start(out=rows[:, 0 : NODE + 1], in_=w1_blocks[block // PACK, block % PACK])
             w1_rows.append(rows)
-            if block == 1:
-                nc.sync.dma_start(out=vectors[0:1, 5 * P : 6 * P], in_=b2.rearrange("(o n) -> o n", o=1))
         w2_rows = keep.tile([P, MID], BF16)
         nc.sync.dma_start(out=w2_rows[:], in_=W2)
 
@@ -184,18 +183,27 @@ def tile_edgenetwork_s_kernel(
                 stop=(c == PASSES - 1),
             )
 
-        def spread_vectors():
+        def spread_row(bank, column):
+            nc.tensor.matmul(
+                out=bank[:, 2 * P : 3 * P],
+                lhsT=ones[:],
+                rhs=vectors[:, column : column + P],
+                start=True,
+                stop=True,
+            )
+
+        def spread_b1_and_edge():
             bank = flip_banks.tile([P, 4 * P], F32)
             b1_words = vectors[:, 0:K_PASS].bitcast(F32)
             for u in range(HALVES):
                 nc.tensor.transpose(bank[:, u * P : (u + 1) * P], b1_words[:, u : HALVES * P : HALVES], identity[:])
-            nc.tensor.matmul(out=bank[:, 2 * P : 4 * P], lhsT=ones[:], rhs=vectors[:, K_PASS:], start=True, stop=True)
+            spread_row(bank, 4 * P)
             for u in range(HALVES):
-                nc.scalar.copy(
+                nc.vector.tensor_copy(
                     out=b1_cols[:].rearrange("p c (u e) -> p u c e", u=HALVES)[:, u],
                     in_=bank[:, u * P : u * P + PASSES].bitcast(BF16).rearrange("p (c e) -> p c e", c=PASSES),
                 )
-            nc.scalar.copy(out=spread[:], in_=bank[:, 2 * P : 4 * P])
+            nc.vector.tensor_copy(out=spread[:, 0:P], in_=bank[:, 2 * P : 3 * P])
 
         flip("x", x_rows, nc.vector.tensor_copy)
         flip(0, w1_rows[0])
@@ -203,9 +211,9 @@ def tile_edgenetwork_s_kernel(
         flip(1, w1_rows[1])
         quantise(0)
         flip(2, w1_rows[2])
-        spread_vectors()
         quantise(1)
         flip(3, w1_rows[3])
+        spread_b1_and_edge()
         quantise(2)
         edge_term(0)
         edge_term(1)
@@ -216,18 +224,22 @@ def tile_edgenetwork_s_kernel(
         flip(5, w1_rows[5])
         for block in range(PACK):
             multiply(block)
+        edge_term(4)
         quantise(4)
         flip(6, w1_rows[6])
-        edge_term(4)
         add_edge_terms(hidden_first[:], 0, PACK)
         quantise(5)
         flip(7, w1_rows[7])
         relu(0)
+        edge_term(5)
         quantise(6)
         quantise_hidden(0)
         flip("w2", w2_rows)
-        for block in range(PACK + 1, BLOCKS):
-            edge_term(block)
+        bank = flip_banks.tile([P, 4 * P], F32)
+        spread_row(bank, 5 * P)
+        nc.scalar.copy(out=spread[:, P : 2 * P], in_=bank[:, 2 * P : 3 * P])
+        edge_term(6)
+        edge_term(7)
         quantise(7)
         for block in range(PACK, BLOCKS):
             multiply(block)

@@ -71,7 +71,11 @@ def tile_edgenetwork_s_kernel(
         w1_rows = []
         for block in range(BLOCKS):
             rows = blocks.tile([P, NODE + 2], BF16, name="w1_rows")
-            nc.sync.dma_start(out=rows[:, 0 : NODE + 1], in_=w1_blocks[block // PACK, block % PACK])
+            cuts = (0, NODE + 1) if block < LAST else (0, K_PASS, NODE + 1)
+            for first, last in zip(cuts, cuts[1:]):
+                nc.sync.dma_start(
+                    out=rows[:, first:last], in_=w1_blocks[block // PACK, block % PACK][:, first:last]
+                )
             w1_rows.append(rows)
         w2_rows = keep.tile([P, MID], BF16)
         nc.sync.dma_start(out=w2_rows[:], in_=W2)
@@ -90,29 +94,34 @@ def tile_edgenetwork_s_kernel(
         hidden_last = banks.tile([P, 1, P], F32)
         out_acc = banks.tile([P, P], F32)
 
-        def flip(key, rows, copy=nc.scalar.copy):
+        def flip(key, rows, copy=nc.scalar.copy, passes=(0, PASSES)):
             words = rows[:, 0:NODE].bitcast(F32)
+            low, high = passes
             bank = flip_banks.tile([P, PASSES * HALVES, P], F32)
-            for q in range(PASSES * HALVES):
+            for q in range(low * HALVES, high * HALVES):
                 g, u = divmod(q, HALVES)
                 first = g * HALVES * P + u
                 nc.tensor.transpose(bank[:, q, :], words[:, first : (g + 1) * HALVES * P : HALVES], identity[:])
-            grouped = blocks.tile([P, PASSES, P, PACK], BF16, align_bytes=64)
+            if low == 0:
+                turned[key] = blocks.tile([P, PASSES, P, PACK], BF16, name="grouped", align_bytes=64)
             copy(
-                out=grouped[:].bitcast(F32),
-                in_=bank[:].rearrange("p (g u) c -> p g c u", u=HALVES),
+                out=turned[key][:, low:high].bitcast(F32),
+                in_=bank[:, low * HALVES : high * HALVES].rearrange("p (g u) c -> p g c u", u=HALVES),
             )
-            turned[key] = grouped
 
-        def quantise(key):
-            codes = blocks.tile([P, PASSES * P], U32, align_bytes=64)
-            scales = blocks.tile([P, PASSES * P], U8, align_bytes=64)
+        def quantise(key, passes=(0, PASSES)):
+            low, high = passes
+            if low == 0:
+                operands[key] = (
+                    blocks.tile([P, PASSES * P], U32, name="codes", align_bytes=64),
+                    blocks.tile([P, PASSES * P], U8, name="scales", align_bytes=64),
+                )
+            codes, scales = operands[key]
             nc.vector.quantize_mx(
-                out=codes[:].bitcast(FP8X4),
-                scales=scales[:],
-                in_=turned[key][:].rearrange("p g c t -> p (g c t)"),
+                out=codes[:, low * P : high * P].bitcast(FP8X4),
+                scales=scales[:, low * P : high * P],
+                in_=turned[key][:, low:high].rearrange("p g c t -> p (g c t)"),
             )
-            operands[key] = (codes, scales)
 
         def multiply(block):
             if block < PACK:
@@ -153,13 +162,20 @@ def tile_edgenetwork_s_kernel(
                 op=ALU.add,
             )
 
-        def relu(c):
+        def relu(c, edges):
             nc.vector.tensor_scalar(
-                out=h_grouped[:, c, :, :],
-                in0=pre[:, c * PACK : (c + 1) * PACK, :].rearrange("p t e -> p e t"),
+                out=h_grouped[:, c, edges, :],
+                in0=pre[:, c * PACK : (c + 1) * PACK, edges].rearrange("p t e -> p e t"),
                 scalar1=0.0,
                 scalar2=None,
                 op0=ALU.max,
+            )
+
+        def relu_scalar(c, edges):
+            nc.scalar.activation(
+                out=h_grouped[:, c, edges, :],
+                in_=pre[:, c * PACK : (c + 1) * PACK, edges].rearrange("p t e -> p e t"),
+                func=ACT.Relu,
             )
 
         def quantise_hidden(c):
@@ -229,8 +245,9 @@ def tile_edgenetwork_s_kernel(
         flip(6, w1_rows[6])
         add_edge_terms(hidden_first[:], 0, PACK)
         quantise(5)
-        flip(7, w1_rows[7])
-        relu(0)
+        flip(7, w1_rows[7], passes=(0, 1))
+        flip(7, w1_rows[7], passes=(1, 2))
+        relu(0, slice(0, P))
         edge_term(5)
         quantise(6)
         quantise_hidden(0)
@@ -240,19 +257,24 @@ def tile_edgenetwork_s_kernel(
         nc.scalar.copy(out=spread[:, P : 2 * P], in_=bank[:, 2 * P : 3 * P])
         edge_term(6)
         edge_term(7)
-        quantise(7)
+        quantise(7, passes=(0, 1))
+        quantise(7, passes=(1, 2))
         for block in range(PACK, BLOCKS):
             multiply(block)
         add_edge_terms(hidden_rest[:], PACK, LAST)
         add_edge_terms(hidden_last[:], LAST, BLOCKS)
         quantise("w2")
-        relu(1)
+        relu(1, slice(0, 80))
+        relu_scalar(1, slice(80, P))
         quantise_hidden(1)
         second_layer(0)
         second_layer(1)
 
         biased = keep.tile([P, P], F32)
-        nc.vector.tensor_tensor(out=biased[:], in0=out_acc[:], in1=spread[:, P : 2 * P], op=ALU.add)
         result = keep.tile([P, P], F32)
-        nc.scalar.activation(out=result[:], in_=biased[:], func=ACT.Tanh)
+        for half in (slice(0, P // 2), slice(P // 2, P)):
+            nc.vector.tensor_tensor(
+                out=biased[:, half], in0=out_acc[:, half], in1=spread[:, P:][:, half], op=ALU.add
+            )
+            nc.scalar.activation(out=result[:, half], in_=biased[:, half], func=ACT.Tanh)
         nc.sync.dma_start(out=out, in_=result[:])

from contextlib import ExitStack

import concourse.mybir as mybir
from concourse.masks import make_identity

F32 = mybir.dt.float32
BF16 = mybir.dt.bfloat16
U32 = mybir.dt.uint32
U8 = mybir.dt.uint8
FP8X4 = mybir.dt.float8_e4m3fn_x4
ALU = mybir.AluOpType
ACT = mybir.ActivationFunctionType

P = 128
PACK = 4
K_PASS = P * PACK
NODE = 1024
MID = 1024
PASSES = NODE // K_PASS
HALVES = 2
BLOCKS = MID // P
LAST = BLOCKS - 1

FLOPS = 2 * P * (NODE + 1) * MID + 2 * P * MID * P


def tile_edgenetwork_s_kernel(
    tc,
    dst_node_feat,
    dst_node_hidden,
    src_node_feat,
    src_node_hidden,
    edge_feat,
    W1,
    b1,
    W2,
    b2,
    out,
):
    nc = tc.nc
    with ExitStack() as ctx:
        keep = ctx.enter_context(tc.tile_pool(name="keep", bufs=1))
        blocks = ctx.enter_context(tc.tile_pool(name="blocks", bufs=BLOCKS + 2))
        flip_banks = ctx.enter_context(tc.psum_pool(name="flip", bufs=4))
        banks = ctx.enter_context(tc.psum_pool(name="banks", bufs=1))
        ctx.enter_context(tc.manual_schedule())

        vectors = keep.tile([P, 6 * P], BF16)
        nc.vector.memset(vectors[:].bitcast(U32), 0)
        table_in = keep.tile([P, 1], F32)
        table_out = keep.tile([P, 1], F32)
        nc.vector.memset(table_in[:], 0.0)
        ones = keep.tile([P, P], BF16)
        nc.vector.memset(ones[:], 1.0)
        identity = keep.tile([P, P], F32)
        make_identity(nc, identity[:])

        x_rows = keep.tile([P, NODE], BF16)
        column = 0
        for part in (dst_node_feat, dst_node_hidden, src_node_feat, src_node_hidden):
            width = part.shape[1]
            nc.sync.dma_start(out=x_rows[:, column : column + width], in_=part)
            column += width

        nc.gpsimd.dma_start(out=vectors[0:PASSES, 0:K_PASS], in_=b1.rearrange("(c q) -> c q", q=K_PASS))
        nc.gpsimd.dma_start(out=vectors[0:1, 5 * P : 6 * P], in_=b2.rearrange("(o n) -> o n", o=1))
        nc.scalar.dma_start(out=vectors[0:1, 4 * P : 5 * P], in_=edge_feat.rearrange("(o e) -> o e", o=1))
        nc.scalar.activation(out=table_out[:], in_=table_in[:], func=ACT.Tanh)

        w1_blocks = W1.rearrange("(c p t) k -> c t p k", p=P, t=PACK)
        w1_rows = []
        for block in range(BLOCKS):
            rows = blocks.tile([P, NODE + 2], BF16, name="w1_rows")
            cuts = (0, NODE + 1) if block < LAST else (0, K_PASS, NODE + 1)
            for first, last in zip(cuts, cuts[1:]):
                nc.sync.dma_start(
                    out=rows[:, first:last], in_=w1_blocks[block // PACK, block % PACK][:, first:last]
                )
            w1_rows.append(rows)
        w2_rows = keep.tile([P, MID], BF16)
        nc.sync.dma_start(out=w2_rows[:], in_=W2)

        turned = {}
        operands = {}
        edge_terms = keep.tile([P, BLOCKS, P], F32)
        b1_cols = keep.tile([P, PASSES, PACK], BF16)
        spread = keep.tile([P, 2 * P], F32)
        pre = keep.tile([P, BLOCKS, P], F32)
        h_grouped = keep.tile([P, PASSES, P, PACK], BF16, align_bytes=64)
        h_codes = keep.tile([P, PASSES * P], U32, align_bytes=64)
        h_scales = keep.tile([P, PASSES * P], U8, align_bytes=64)
        hidden_first = banks.tile([P, PACK, P], F32)
        hidden_rest = banks.tile([P, PACK - 1, P], F32)
        hidden_last = banks.tile([P, 1, P], F32)
        out_acc = banks.tile([P, P], F32)

        def flip(key, rows, copy=nc.scalar.copy, passes=(0, PASSES)):
            words = rows[:, 0:NODE].bitcast(F32)
            low, high = passes
            bank = flip_banks.tile([P, PASSES * HALVES, P], F32)
            for q in range(low * HALVES, high * HALVES):
                g, u = divmod(q, HALVES)
                first = g * HALVES * P + u
                nc.tensor.transpose(bank[:, q, :], words[:, first : (g + 1) * HALVES * P : HALVES], identity[:])
            if low == 0:
                turned[key] = blocks.tile([P, PASSES, P, PACK], BF16, name="grouped", align_bytes=64)
            copy(
                out=turned[key][:, low:high].bitcast(F32),
                in_=bank[:, low * HALVES : high * HALVES].rearrange("p (g u) c -> p g c u", u=HALVES),
            )

        def quantise(key, passes=(0, PASSES)):
            low, high = passes
            if low == 0:
                operands[key] = (
                    blocks.tile([P, PASSES * P], U32, name="codes", align_bytes=64),
                    blocks.tile([P, PASSES * P], U8, name="scales", align_bytes=64),
                )
            codes, scales = operands[key]
            nc.vector.quantize_mx(
                out=codes[:, low * P : high * P].bitcast(FP8X4),
                scales=scales[:, low * P : high * P],
                in_=turned[key][:, low:high].rearrange("p g c t -> p (g c t)"),
            )

        def multiply(block):
            if block < PACK:
                acc = hidden_first[:, block, :]
            elif block < LAST:
                acc = hidden_rest[:, block - PACK, :]
            else:
                acc = hidden_last[:, 0, :]
            w1_codes, w1_scales = operands[block]
            x_codes, x_scales = operands["x"]
            for g in range(PASSES):
                cols = slice(g * P, (g + 1) * P)
                nc.tensor.matmul_mx(
                    out=acc,
                    lhsT=w1_codes[:, cols].bitcast(FP8X4),
                    lhsT_scale=w1_scales[:, cols],
                    rhs=x_codes[:, cols].bitcast(FP8X4),
                    rhs_scale=x_scales[:, cols],
                    start=(g == 0),
                    stop=(g == PASSES - 1),
                )

        def edge_term(block):
            nc.vector.tensor_scalar(
                out=edge_terms[:, block, :],
                in0=spread[:, 0:P],
                scalar1=w1_rows[block][:, NODE : NODE + 1],
                scalar2=b1_cols[:, block // PACK, block % PACK : block % PACK + 1],
                op0=ALU.mult,
                op1=ALU.add,
            )

        def add_edge_terms(acc, first, last):
            nc.vector.tensor_tensor(
                out=pre[:, first:last, :],
                in0=acc,
                in1=edge_terms[:, first:last, :],
                op=ALU.add,
            )

        def relu(c, edges):
            nc.vector.tensor_scalar(
                out=h_grouped[:, c, edges, :],
                in0=pre[:, c * PACK : (c + 1) * PACK, edges].rearrange("p t e -> p e t"),
                scalar1=0.0,
                scalar2=None,
                op0=ALU.max,
            )

        def relu_scalar(c, edges):
            nc.scalar.activation(
                out=h_grouped[:, c, edges, :],
                in_=pre[:, c * PACK : (c + 1) * PACK, edges].rearrange("p t e -> p e t"),
                func=ACT.Relu,
            )

        def quantise_hidden(c):
            cols = slice(c * P, (c + 1) * P)
            nc.vector.quantize_mx(
                out=h_codes[:, cols].bitcast(FP8X4),
                scales=h_scales[:, cols],
                in_=h_grouped[:, c, :, :].rearrange("p e t -> p (e t)"),
            )

        def second_layer(c):
            w2_codes, w2_scales = operands["w2"]
            cols = slice(c * P, (c + 1) * P)
            nc.tensor.matmul_mx(
                out=out_acc[:],
                lhsT=h_codes[:, cols].bitcast(FP8X4),
                lhsT_scale=h_scales[:, cols],
                rhs=w2_codes[:, cols].bitcast(FP8X4),
                rhs_scale=w2_scales[:, cols],
                start=(c == 0),
                stop=(c == PASSES - 1),
            )

        def spread_row(bank, column):
            nc.tensor.matmul(
                out=bank[:, 2 * P : 3 * P],
                lhsT=ones[:],
                rhs=vectors[:, column : column + P],
                start=True,
                stop=True,
            )

        def spread_b1_and_edge():
            bank = flip_banks.tile([P, 4 * P], F32)
            b1_words = vectors[:, 0:K_PASS].bitcast(F32)
            for u in range(HALVES):
                nc.tensor.transpose(bank[:, u * P : (u + 1) * P], b1_words[:, u : HALVES * P : HALVES], identity[:])
            spread_row(bank, 4 * P)
            for u in range(HALVES):
                nc.vector.tensor_copy(
                    out=b1_cols[:].rearrange("p c (u e) -> p u c e", u=HALVES)[:, u],
                    in_=bank[:, u * P : u * P + PASSES].bitcast(BF16).rearrange("p (c e) -> p c e", c=PASSES),
                )
            nc.vector.tensor_copy(out=spread[:, 0:P], in_=bank[:, 2 * P : 3 * P])

        flip("x", x_rows, nc.vector.tensor_copy)
        flip(0, w1_rows[0])
        quantise("x")
        flip(1, w1_rows[1])
        quantise(0)
        flip(2, w1_rows[2])
        quantise(1)
        flip(3, w1_rows[3])
        spread_b1_and_edge()
        quantise(2)
        edge_term(0)
        edge_term(1)
        flip(4, w1_rows[4])
        edge_term(2)
        quantise(3)
        edge_term(3)
        flip(5, w1_rows[5])
        for block in range(PACK):
            multiply(block)
        edge_term(4)
        quantise(4)
        flip(6, w1_rows[6])
        add_edge_terms(hidden_first[:], 0, PACK)
        quantise(5)
        flip(7, w1_rows[7], passes=(0, 1))
        flip(7, w1_rows[7], passes=(1, 2))
        relu(0, slice(0, P))
        edge_term(5)
        quantise(6)
        quantise_hidden(0)
        flip("w2", w2_rows)
        bank = flip_banks.tile([P, 4 * P], F32)
        spread_row(bank, 5 * P)
        nc.scalar.copy(out=spread[:, P : 2 * P], in_=bank[:, 2 * P : 3 * P])
        edge_term(6)
        edge_term(7)
        quantise(7, passes=(0, 1))
        quantise(7, passes=(1, 2))
        for block in range(PACK, BLOCKS):
            multiply(block)
        add_edge_terms(hidden_rest[:], PACK, LAST)
        add_edge_terms(hidden_last[:], LAST, BLOCKS)
        quantise("w2")
        relu(1, slice(0, 80))
        relu_scalar(1, slice(80, P))
        quantise_hidden(1)
        second_layer(0)
        second_layer(1)

        biased = keep.tile([P, P], F32)
        result = keep.tile([P, P], F32)
        for half in (slice(0, P // 2), slice(P // 2, P)):
            nc.vector.tensor_tensor(
                out=biased[:, half], in0=out_acc[:, half], in1=spread[:, P:][:, half], op=ALU.add
            )
            nc.scalar.activation(out=result[:, half], in_=biased[:, half], func=ACT.Tanh)
        nc.sync.dma_start(out=out, in_=result[:])
